import numpy as np
import ml_dtypes


def mxq(x, axis, fmt="e4m3"):
    dtype, down = {"e4m3": (ml_dtypes.float8_e4m3fn, 7), "e5m2": (ml_dtypes.float8_e5m2, 14)}[fmt]
    v = np.moveaxis(np.asarray(x, np.float32).astype(ml_dtypes.bfloat16).astype(np.float64), axis, -1)
    blocks = v.reshape(v.shape[:-1] + (-1, 32))
    amax = np.abs(blocks).max(-1, keepdims=True)
    byte = np.maximum(np.where(amax > 0, np.frexp(amax)[1] - 1 + 127, 0) - down, 1)
    scale = np.exp2(byte - 127.0)
    codes = (blocks / scale).astype(np.float32).astype(dtype).astype(np.float64)
    return np.moveaxis((codes * scale).reshape(v.shape), -1, axis)


WIDE = False


def mx_kscale(k):
    if not WIDE:
        return np.ones(k)
    levels = np.array([10, -10, 5, -5, 0])
    a = np.random.permutation(np.resize(levels, k // 512 * 4)).reshape(k // 512, 4)
    idx = np.arange(k)
    return np.exp2(a[idx // 512, idx % 128 // 32])


BF16 = ml_dtypes.bfloat16


def bf(x):
    return np.asarray(x, np.float32).astype(BF16)


def f64(x):
    return np.asarray(x).astype(np.float64)


E2M1 = np.array([0.0, 0.5, 1.0, 1.5, 2.0, 3.0, 4.0, 6.0, -0.0, -0.5, -1.0, -1.5, -2.0, -3.0, -4.0, -6.0])


def pack_weight(w, fmt):
    k, n = w.shape
    w = f64(bf(w)).reshape(k // 32, 32, n)
    amax = np.abs(w).max(1)
    if fmt == "e4m3":
        byte = np.frexp(amax)[1] - 1 + 127 - 7
    else:
        mant, ex = np.frexp(amax / 6.0)
        byte = np.where(mant > 0.5, ex, ex - 1) + 127
    byte = np.clip(np.where(amax > 0, byte, 1), 1, 254)
    scaled = (w * np.exp2(127.0 - byte)[:, None, :]).reshape(k, n).astype(np.float32)
    by_word = np.ascontiguousarray(scaled.reshape(k // 512, 128, 4, n).transpose(0, 1, 3, 2))
    if fmt == "e4m3":
        words = by_word.astype(ml_dtypes.float8_e4m3fn).view(np.uint8)
    else:
        c = by_word.astype(ml_dtypes.float4_e2m1fn).view(np.uint8) & 0xF
        words = c[..., 0::2] | (c[..., 1::2] << 4)
    return np.ascontiguousarray(words), np.ascontiguousarray(byte.astype(np.uint8).reshape(k // 512, 16, n))


def unpack_weight(words, scales, fmt):
    g, p, n, _ = words.shape
    if fmt == "e4m3":
        vals = np.ascontiguousarray(words).view(ml_dtypes.float8_e4m3fn).astype(np.float64)
    else:
        nib = np.empty((g, p, n, 4), np.uint8)
        nib[..., 0::2] = words & 0xF
        nib[..., 1::2] = words >> 4
        vals = E2M1[nib]
    vals = vals * np.repeat(np.exp2(scales.astype(np.float64) - 127.0), 8, axis=1)[..., None]
    return vals.transpose(0, 1, 3, 2).reshape(g * 512, n)


B, C, IN, H, ND, NG, NL = 32, 128, 512, 256, 2, 4, 2
N = B * C
USED = [0, 2, 3]


def sigmoid(v):
    return 1.0 / (1.0 + np.exp(-v))


def cell(inq, wt, b1, b2):
    wu = wt.reshape(-1, NG, H)[:, USED].reshape(-1, len(USED) * H)
    gates = (inq @ wu) + b1.reshape(NG, H)[USED].reshape(-1) + b2.reshape(NG, H)[USED].reshape(-1)
    i, g, o = np.split(gates, len(USED), axis=-1)
    c = sigmoid(i) * np.tanh(g)
    return sigmoid(o) * np.tanh(c)


def setup_inputs():
    s = mx_kscale(IN)
    x = bf(np.random.standard_normal((B, C, IN)) * s)
    w = np.random.standard_normal((ND, NG * H, IN)) * 1.5 / np.sqrt(IN) / s
    cat = np.ascontiguousarray(w.swapaxes(1, 2)).reshape(-1, NG * H)
    words, scales = pack_weight(cat, "e4m3")
    return {"x": x,
            "w_ih_words": words,
            "w_ih_scales": scales,
            "b_ih": bf(np.random.standard_normal((ND, NG * H)) * 0.3),
            "b_hh": bf(np.random.standard_normal((ND, NG * H)) * 0.3)}


def reference(x, w_ih_words, w_ih_scales, b_ih, b_hh):
    xq = mxq(f64(x).reshape(N, IN), 1, "e4m3")
    w = unpack_weight(w_ih_words, w_ih_scales, "e4m3").reshape(ND, IN, NG * H)
    b1, b2 = f64(b_ih), f64(b_hh)
    return np.concatenate([cell(xq, w[d], b1[d], b2[d]) for d in range(ND)], axis=-1)

@@ -1,0 +1,233 @@
+from contextlib import ExitStack
+
+import concourse.mybir as mybir
+from concourse.masks import make_identity
+
+F32 = mybir.dt.float32
+BF16 = mybir.dt.bfloat16
+I32 = mybir.dt.int32
+U32 = mybir.dt.uint32
+U8 = mybir.dt.uint8
+FP8X4 = mybir.dt.float8_e4m3fn_x4
+ACT = mybir.ActivationFunctionType
+ALU = mybir.AluOpType
+
+P = 128
+PACK = 4
+K = P * PACK
+PAIRS = K // 2
+ROWS = 4096
+CHUNK = 512
+ROW_TILES = CHUNK // P
+CHUNKS = ROWS // CHUNK
+DIRS = 2
+H = 256
+GATE_COLS = 4 * H
+I_BLOCK, G_BLOCK, O_BLOCK = 0, 2, 3
+COL_TILES = DIRS * H // P
+STEPS = CHUNKS * COL_TILES
+BIAS_ROWS = DIRS * GATE_COLS // P
+
+FLOPS = 2 * ROWS * K * DIRS * 3 * H
+BYTES = ROWS * K * 2 + DIRS * 3 * H * (K + K // 32 + 2 * 2) + ROWS * DIRS * H * 4
+
+
+def tile_lstmnetwork_pa_t_e_kernel(tc, x, w_ih_words, w_ih_scales, b_ih, b_hh, out):
+    nc = tc.nc
+
+    x_rows = x.rearrange("b c k -> (b c) k").rearrange("(c p r) k -> c p (r k)", p=P, r=ROW_TILES)
+    out_rows = out.rearrange("(c p r) n -> c p r n", p=P, r=ROW_TILES)
+
+    with ExitStack() as ctx:
+        ctx.enter_context(tc.manual_schedule())
+        const = ctx.enter_context(tc.tile_pool(name="const", bufs=1))
+        quantised = ctx.enter_context(tc.tile_pool(name="quantised", bufs=2))
+        work = ctx.enter_context(tc.tile_pool(name="work", bufs=2))
+        held = ctx.enter_context(tc.tile_pool(name="held", bufs=3))
+        stage = ctx.enter_context(tc.tile_pool(name="stage", bufs=3))
+        gate_psum = ctx.enter_context(tc.psum_pool(name="gate_psum", bufs=5))
+        turn_psum = ctx.enter_context(tc.psum_pool(name="turn_psum", bufs=3))
+
+        x_sb = []
+        for c in range(CHUNKS):
+            x_chunk = const.tile([P, ROW_TILES * K], BF16, name="x_chunk%d" % c)
+            x_sb.append(x_chunk)
+        nc.sync.dma_start(out=x_sb[0][:], in_=x_rows[0])
+
+        w_planes = const.tile([P, DIRS, GATE_COLS], U8, align_bytes=64)
+        nc.vector.memset(w_planes[:].bitcast(I32), 0)
+        scale_rows = w_ih_scales.rearrange("d q n -> q d n")
+        for quadrant in range(4):
+            nc.sync.dma_start(
+                out=w_planes[32 * quadrant : 32 * quadrant + 4, :, :].bitcast(I32),
+                in_=scale_rows[4 * quadrant : 4 * quadrant + 4].bitcast(I32),
+            )
+
+        w_codes = const.tile([P, DIRS, GATE_COLS], U32, align_bytes=64)
+        code_bytes = w_ih_words.rearrange("d p n t -> p d (n t)")
+        for first_block, last_block in ((I_BLOCK, I_BLOCK), (G_BLOCK, O_BLOCK)):
+            cols = slice(first_block * H, (last_block + 1) * H)
+            byte_cols = slice(first_block * H * PACK, (last_block + 1) * H * PACK)
+            nc.sync.dma_start(
+                out=w_codes[:, :, cols].bitcast(I32), in_=code_bytes[:, :, byte_cols].bitcast(I32)
+            )
+
+        for c in range(1, CHUNKS):
+            nc.sync.dma_start(out=x_sb[c][:], in_=x_rows[c])
+
+        ident = const.tile([P, P], F32)
+        make_identity(nc, ident[:])
+
+        b_ih_rows = const.tile([BIAS_ROWS, P], BF16)
+        b_hh_rows = const.tile([BIAS_ROWS, P], BF16)
+        nc.scalar.dma_start(out=b_ih_rows[:], in_=b_ih.rearrange("d (t c) -> (d t) c", c=P))
+        nc.scalar.dma_start(out=b_hh_rows[:], in_=b_hh.rearrange("d (t c) -> (d t) c", c=P))
+        bias_rows = const.tile([P, P], F32)
+        nc.vector.memset(bias_rows[:], 0.0)
+        nc.vector.tensor_tensor(
+            out=bias_rows[0:BIAS_ROWS, :], in0=b_ih_rows[:], in1=b_hh_rows[:], op=ALU.add
+        )
+        bias = const.tile([P, BIAS_ROWS], F32)
+
+        turned_x = {}
+        grouped = {}
+        x_mx = {}
+        gates = {}
+        sig_i, tanh_g, sig_o, cell, tanh_c, hidden, turned_h = {}, {}, {}, {}, {}, {}, {}
+        out_sb = {}
+
+        def transpose_x(c, half):
+            x_words = x_sb[c][:].bitcast(F32)
+            planes = turn_psum.tile([P, 2, 2 * P], F32, tag="turn")
+            for t in range(2):
+                first_word = (2 * half + t) * PAIRS
+                for u in range(2):
+                    nc.tensor.transpose(
+                        planes[:, u, t * P : (t + 1) * P],
+                        x_words[:, first_word + u : first_word + PAIRS : 2],
+                        ident[:],
+                    )
+            turned_x[(c, half)] = planes
+
+        def regroup_x(c, half):
+            if half == 0:
+                in_order = quantised.tile([P, CHUNK * PACK], BF16, align_bytes=64)
+                grouped[c] = in_order
+            half_words = 2 * (CHUNK // 2)
+            words = grouped[c][:].bitcast(F32)[:, half * half_words : (half + 1) * half_words]
+            nc.vector.tensor_copy(
+                out=words.rearrange("p (row u) -> p row u", u=2),
+                in_=turned_x[(c, half)][:].rearrange("p u row -> p row u"),
+            )
+
+        def quantise_x(c):
+            codes = quantised.tile([P, CHUNK], U32, align_bytes=64)
+            plane = quantised.tile([P, CHUNK], U8, align_bytes=64)
+            nc.vector.quantize_mx(out=codes[:].bitcast(FP8X4), scales=plane[:], in_=grouped[c][:])
+            x_mx[c] = (codes, plane)
+
+        def place(s):
+            return s // COL_TILES, (s % COL_TILES) // 2, s % 2
+
+        def multiply(s):
+            c, d, half = place(s)
+            codes, plane = x_mx[c]
+            banks = []
+            for block in (I_BLOCK, G_BLOCK, O_BLOCK):
+                cols = slice(block * H + half * P, block * H + (half + 1) * P)
+                bank = gate_psum.tile([P, CHUNK], F32, tag="gate")
+                nc.tensor.matmul_mx(
+                    out=bank[:],
+                    lhsT=w_codes[:, d, cols].bitcast(FP8X4),
+                    lhsT_scale=w_planes[:, d, cols],
+                    rhs=codes[:].bitcast(FP8X4),
+                    rhs_scale=plane[:],
+                    start=True,
+                    stop=True,
+                )
+                banks.append(bank)
+            gates[s] = banks
+
+        def activate_gates(s):
+            c, d, half = place(s)
+            bank_i, bank_g, bank_o = gates[s]
+
+            def bias_of(block):
+                t = (d * GATE_COLS + block * H + half * P) // P
+                return bias[:, t : t + 1]
+
+            s_i = work.tile([P, CHUNK], F32)
+            nc.scalar.activation(out=s_i[:], in_=bank_i[:], func=ACT.Sigmoid, bias=bias_of(I_BLOCK))
+            t_g = work.tile([P, CHUNK], F32)
+            nc.scalar.activation(out=t_g[:], in_=bank_g[:], func=ACT.Tanh, bias=bias_of(G_BLOCK))
+            s_o = held.tile([P, CHUNK], F32)
+            nc.scalar.activation(out=s_o[:], in_=bank_o[:], func=ACT.Sigmoid, bias=bias_of(O_BLOCK))
+            sig_i[s], tanh_g[s], sig_o[s] = s_i, t_g, s_o
+
+        def cell_state(s):
+            c_new = work.tile([P, CHUNK], F32)
+            nc.vector.tensor_tensor(out=c_new[:], in0=sig_i[s][:], in1=tanh_g[s][:], op=ALU.mult)
+            cell[s] = c_new
+
+        def activate_cell(s):
+            t_c = work.tile([P, CHUNK], F32)
+            nc.scalar.activation(out=t_c[:], in_=cell[s][:], func=ACT.Tanh)
+            tanh_c[s] = t_c
+
+        def hidden_state(s):
+            h_t = work.tile([P, CHUNK], F32)
+            nc.vector.tensor_tensor(out=h_t[:], in0=sig_o[s][:], in1=tanh_c[s][:], op=ALU.mult)
+            hidden[s] = h_t
+
+        def transpose_h(s):
+            h_rows = turn_psum.tile([P, ROW_TILES, P], F32, tag="turn")
+            for r in range(ROW_TILES):
+                nc.tensor.transpose(h_rows[:, r, :], hidden[s][:, r * P : (r + 1) * P], ident[:])
+            turned_h[s] = h_rows
+
+        def store(s):
+            c, d, half = place(s)
+            if half == 0:
+                h_out = stage.tile([P, ROW_TILES, H], F32)
+                out_sb[(c, d)] = h_out
+            nc.vector.tensor_copy(
+                out=out_sb[(c, d)][:, :, half * P : (half + 1) * P], in_=turned_h[s][:]
+            )
+            if half == 1:
+                nc.sync.dma_start(
+                    out=out_rows[c][:, :, d * H : (d + 1) * H], in_=out_sb[(c, d)][:]
+                )
+
+        transpose_x(0, 0)
+        transpose_x(0, 1)
+        bias_turned = turn_psum.tile([P, P], F32, tag="turn")
+        nc.tensor.transpose(bias_turned[:], bias_rows[:], ident[:])
+        regroup_x(0, 0)
+        regroup_x(0, 1)
+        nc.vector.tensor_copy(out=bias[:], in_=bias_turned[:, 0:BIAS_ROWS])
+        quantise_x(0)
+
+        for s in range(-1, STEPS + 3):
+            next_chunk, piece = (s + 1) // COL_TILES + 1, (s + 1) % COL_TILES
+            prepare = next_chunk < CHUNKS
+
+            if 0 <= s < STEPS:
+                activate_gates(s)
+            if 0 <= s - 1 < STEPS:
+                activate_cell(s - 1)
+            if prepare and piece == 3:
+                quantise_x(next_chunk)
+            if s + 1 < STEPS:
+                multiply(s + 1)
+            if 0 <= s - 2 < STEPS:
+                hidden_state(s - 2)
+            if 0 <= s - 3 < STEPS:
+                store(s - 3)
+            if prepare and piece in (1, 2):
+                regroup_x(next_chunk, piece - 1)
+            if 0 <= s - 2 < STEPS:
+                transpose_h(s - 2)
+            if prepare and piece in (0, 1):
+                transpose_x(next_chunk, piece)
+            if 0 <= s < STEPS:
+                cell_state(s)

@@ -26,6 +26,7 @@ GATE_COLS = 4 * H
 I_BLOCK, G_BLOCK, O_BLOCK = 0, 2, 3
 COL_TILES = DIRS * H // P
 STEPS = CHUNKS * COL_TILES
+STORE_LAG = 3
 BIAS_ROWS = DIRS * GATE_COLS // P
 
 FLOPS = 2 * ROWS * K * DIRS * 3 * H
@@ -44,15 +45,19 @@ def tile_lstmnetwork_pa_t_e_kernel(tc, x, w_ih_words, w_ih_scales, b_ih, b_hh, o
         quantised = ctx.enter_context(tc.tile_pool(name="quantised", bufs=2))
         work = ctx.enter_context(tc.tile_pool(name="work", bufs=2))
         held = ctx.enter_context(tc.tile_pool(name="held", bufs=3))
-        stage = ctx.enter_context(tc.tile_pool(name="stage", bufs=3))
+        stage = ctx.enter_context(tc.tile_pool(name="stage", bufs=4))
         gate_psum = ctx.enter_context(tc.psum_pool(name="gate_psum", bufs=5))
         turn_psum = ctx.enter_context(tc.psum_pool(name="turn_psum", bufs=3))
 
-        x_sb = []
-        for c in range(CHUNKS):
-            x_chunk = const.tile([P, ROW_TILES * K], BF16, name="x_chunk%d" % c)
-            x_sb.append(x_chunk)
-        nc.sync.dma_start(out=x_sb[0][:], in_=x_rows[0])
+        x_sb = {}
+
+        def load_x(c):
+            for half in range(2):
+                x_half = const.tile([P, 2 * K], BF16, name="x_%d_%d" % (c, half))
+                nc.sync.dma_start(out=x_half[:], in_=x_rows[c][:, half * 2 * K : (half + 1) * 2 * K])
+                x_sb[(c, half)] = x_half
+
+        load_x(0)
 
         w_planes = const.tile([P, DIRS, GATE_COLS], U8, align_bytes=64)
         nc.vector.memset(w_planes[:].bitcast(I32), 0)
@@ -64,16 +69,17 @@ def tile_lstmnetwork_pa_t_e_kernel(tc, x, w_ih_words, w_ih_scales, b_ih, b_hh, o
             )
 
         w_codes = const.tile([P, DIRS, GATE_COLS], U32, align_bytes=64)
-        code_bytes = w_ih_words.rearrange("d p n t -> p d (n t)")
-        for first_block, last_block in ((I_BLOCK, I_BLOCK), (G_BLOCK, O_BLOCK)):
-            cols = slice(first_block * H, (last_block + 1) * H)
-            byte_cols = slice(first_block * H * PACK, (last_block + 1) * H * PACK)
-            nc.sync.dma_start(
-                out=w_codes[:, :, cols].bitcast(I32), in_=code_bytes[:, :, byte_cols].bitcast(I32)
-            )
+        for d in range(DIRS):
+            code_bytes = w_ih_words[d].rearrange("p n t -> p (n t)")
+            for first_block, last_block in ((I_BLOCK, I_BLOCK), (G_BLOCK, O_BLOCK)):
+                cols = slice(first_block * H, (last_block + 1) * H)
+                byte_cols = slice(first_block * H * PACK, (last_block + 1) * H * PACK)
+                nc.sync.dma_start(
+                    out=w_codes[:, d, cols].bitcast(I32), in_=code_bytes[:, byte_cols].bitcast(I32)
+                )
 
         for c in range(1, CHUNKS):
-            nc.sync.dma_start(out=x_sb[c][:], in_=x_rows[c])
+            load_x(c)
 
         ident = const.tile([P, P], F32)
         make_identity(nc, ident[:])
@@ -94,13 +100,12 @@ def tile_lstmnetwork_pa_t_e_kernel(tc, x, w_ih_words, w_ih_scales, b_ih, b_hh, o
         x_mx = {}
         gates = {}
         sig_i, tanh_g, sig_o, cell, tanh_c, hidden, turned_h = {}, {}, {}, {}, {}, {}, {}
-        out_sb = {}
 
         def transpose_x(c, half):
-            x_words = x_sb[c][:].bitcast(F32)
+            x_words = x_sb[(c, half)][:].bitcast(F32)
             planes = turn_psum.tile([P, 2, 2 * P], F32, tag="turn")
             for t in range(2):
-                first_word = (2 * half + t) * PAIRS
+                first_word = t * PAIRS
                 for u in range(2):
                     nc.tensor.transpose(
                         planes[:, u, t * P : (t + 1) * P],
@@ -186,17 +191,13 @@ def tile_lstmnetwork_pa_t_e_kernel(tc, x, w_ih_words, w_ih_scales, b_ih, b_hh, o
             turned_h[s] = h_rows
 
         def store(s):
-            c, d, half = place(s)
-            if half == 0:
-                h_out = stage.tile([P, ROW_TILES, H], F32)
-                out_sb[(c, d)] = h_out
-            nc.vector.tensor_copy(
-                out=out_sb[(c, d)][:, :, half * P : (half + 1) * P], in_=turned_h[s][:]
-            )
-            if half == 1:
-                nc.sync.dma_start(
-                    out=out_rows[c][:, :, d * H : (d + 1) * H], in_=out_sb[(c, d)][:]
-                )
+            h_out = stage.tile([P, ROW_TILES, P], F32)
+            if s < STEPS - STORE_LAG:
+                nc.vector.tensor_copy(out=h_out[:], in_=turned_h[s][:])
+            else:
+                nc.scalar.copy(out=h_out[:], in_=turned_h[s][:])
+            first_col = (s % COL_TILES) * P
+            nc.sync.dma_start(out=out_rows[s // COL_TILES][:, :, first_col : first_col + P], in_=h_out[:])
 
         transpose_x(0, 0)
         transpose_x(0, 1)
@@ -207,7 +208,7 @@ def tile_lstmnetwork_pa_t_e_kernel(tc, x, w_ih_words, w_ih_scales, b_ih, b_hh, o
         nc.vector.tensor_copy(out=bias[:], in_=bias_turned[:, 0:BIAS_ROWS])
         quantise_x(0)
 
-        for s in range(-1, STEPS + 3):
+        for s in range(-1, STEPS + STORE_LAG):
             next_chunk, piece = (s + 1) // COL_TILES + 1, (s + 1) % COL_TILES
             prepare = next_chunk < CHUNKS
 
@@ -221,8 +222,8 @@ def tile_lstmnetwork_pa_t_e_kernel(tc, x, w_ih_words, w_ih_scales, b_ih, b_hh, o
                 multiply(s + 1)
             if 0 <= s - 2 < STEPS:
                 hidden_state(s - 2)
-            if 0 <= s - 3 < STEPS:
-                store(s - 3)
+            if 0 <= s - STORE_LAG < STEPS:
+                store(s - STORE_LAG)
             if prepare and piece in (1, 2):
                 regroup_x(next_chunk, piece - 1)
             if 0 <= s - 2 < STEPS:

@@ -24,10 +24,13 @@ DIRS = 2
 H = 256
 GATE_COLS = 4 * H
 I_BLOCK, G_BLOCK, O_BLOCK = 0, 2, 3
+USED_BLOCKS = (I_BLOCK, G_BLOCK, O_BLOCK)
 COL_TILES = DIRS * H // P
 STEPS = CHUNKS * COL_TILES
 STORE_LAG = 3
 BIAS_ROWS = DIRS * GATE_COLS // P
+FIRST_PIECES = ((0, 1), (1, 1), (2, 2))
+FIRST_GATES = ((0, 0, 1), (0, 1, 1), (1, 0, 2), (0, 2, 2), (1, 2, 2))
 
 FLOPS = 2 * ROWS * K * DIRS * 3 * H
 BYTES = ROWS * K * 2 + DIRS * 3 * H * (K + K // 32 + 2 * 2) + ROWS * DIRS * H * 4
@@ -51,13 +54,18 @@ def tile_lstmnetwork_pa_t_e_kernel(tc, x, w_ih_words, w_ih_scales, b_ih, b_hh, o
 
         x_sb = {}
 
-        def load_x(c):
-            for half in range(2):
-                x_half = const.tile([P, 2 * K], BF16, name="x_%d_%d" % (c, half))
-                nc.sync.dma_start(out=x_half[:], in_=x_rows[c][:, half * 2 * K : (half + 1) * 2 * K])
-                x_sb[(c, half)] = x_half
+        def load_x(c, half):
+            x_half = const.tile([P, 2 * K], BF16, name="x_%d_%d" % (c, half))
+            nc.sync.dma_start(out=x_half[:], in_=x_rows[c][:, half * 2 * K : (half + 1) * 2 * K])
+            x_sb[(c, half)] = x_half
 
-        load_x(0)
+        b_ih_rows = const.tile([BIAS_ROWS, P], BF16)
+        b_hh_rows = const.tile([BIAS_ROWS, P], BF16)
+        nc.sync.dma_start(out=b_ih_rows[:], in_=b_ih.rearrange("d (t c) -> (d t) c", c=P))
+        nc.sync.dma_start(out=b_hh_rows[:], in_=b_hh.rearrange("d (t c) -> (d t) c", c=P))
+
+        load_x(0, 0)
+        load_x(0, 1)
 
         w_planes = const.tile([P, DIRS, GATE_COLS], U8, align_bytes=64)
         nc.vector.memset(w_planes[:].bitcast(I32), 0)
@@ -68,26 +76,27 @@ def tile_lstmnetwork_pa_t_e_kernel(tc, x, w_ih_words, w_ih_scales, b_ih, b_hh, o
                 in_=scale_rows[4 * quadrant : 4 * quadrant + 4].bitcast(I32),
             )
 
-        w_codes = const.tile([P, DIRS, GATE_COLS], U32, align_bytes=64)
-        for d in range(DIRS):
-            code_bytes = w_ih_words[d].rearrange("p n t -> p (n t)")
-            for first_block, last_block in ((I_BLOCK, I_BLOCK), (G_BLOCK, O_BLOCK)):
-                cols = slice(first_block * H, (last_block + 1) * H)
-                byte_cols = slice(first_block * H * PACK, (last_block + 1) * H * PACK)
-                nc.sync.dma_start(
-                    out=w_codes[:, d, cols].bitcast(I32), in_=code_bytes[:, byte_cols].bitcast(I32)
-                )
+        w_codes = {}
 
+        def load_codes(d, half):
+            codes = const.tile([P, len(USED_BLOCKS), P], U32, name="w_%d_%d" % (d, half), align_bytes=64)
+            blocks_dram = w_ih_words[d].rearrange("p n t -> p (n t)").bitcast(I32).rearrange("p (b n) -> p b n", n=H)
+            cols = slice(half * P, (half + 1) * P)
+            nc.sync.dma_start(out=codes[:, 0, :].bitcast(I32), in_=blocks_dram[:, I_BLOCK, cols])
+            nc.sync.dma_start(out=codes[:, 1:3, :].bitcast(I32), in_=blocks_dram[:, G_BLOCK : O_BLOCK + 1, cols])
+            w_codes[(d, half)] = codes
+
+        load_codes(0, 0)
+        load_codes(0, 1)
+        load_codes(1, 0)
+        load_codes(1, 1)
         for c in range(1, CHUNKS):
-            load_x(c)
+            load_x(c, 0)
+            load_x(c, 1)
 
         ident = const.tile([P, P], F32)
         make_identity(nc, ident[:])
 
-        b_ih_rows = const.tile([BIAS_ROWS, P], BF16)
-        b_hh_rows = const.tile([BIAS_ROWS, P], BF16)
-        nc.scalar.dma_start(out=b_ih_rows[:], in_=b_ih.rearrange("d (t c) -> (d t) c", c=P))
-        nc.scalar.dma_start(out=b_hh_rows[:], in_=b_hh.rearrange("d (t c) -> (d t) c", c=P))
         bias_rows = const.tile([P, P], F32)
         nc.vector.memset(bias_rows[:], 0.0)
         nc.vector.tensor_tensor(
@@ -101,73 +110,88 @@ def tile_lstmnetwork_pa_t_e_kernel(tc, x, w_ih_words, w_ih_scales, b_ih, b_hh, o
         gates = {}
         sig_i, tanh_g, sig_o, cell, tanh_c, hidden, turned_h = {}, {}, {}, {}, {}, {}, {}
 
-        def transpose_x(c, half):
-            x_words = x_sb[(c, half)][:].bitcast(F32)
-            planes = turn_psum.tile([P, 2, 2 * P], F32, tag="turn")
-            for t in range(2):
-                first_word = t * PAIRS
+        def transpose_x(c, first, tiles):
+            x_words = x_sb[(c, first // 2)][:].bitcast(F32)
+            planes = turn_psum.tile([P, 2, tiles * P], F32, tag="turn")
+            for t in range(tiles):
+                first_word = ((first + t) % 2) * PAIRS
                 for u in range(2):
                     nc.tensor.transpose(
                         planes[:, u, t * P : (t + 1) * P],
                         x_words[:, first_word + u : first_word + PAIRS : 2],
                         ident[:],
                     )
-            turned_x[(c, half)] = planes
+            turned_x[(c, first)] = planes
 
-        def regroup_x(c, half):
-            if half == 0:
+        def regroup_x(c, first, tiles):
+            if first == 0:
                 in_order = quantised.tile([P, CHUNK * PACK], BF16, align_bytes=64)
                 grouped[c] = in_order
-            half_words = 2 * (CHUNK // 2)
-            words = grouped[c][:].bitcast(F32)[:, half * half_words : (half + 1) * half_words]
+            words = grouped[c][:].bitcast(F32)[:, first * 2 * P : (first + tiles) * 2 * P]
             nc.vector.tensor_copy(
                 out=words.rearrange("p (row u) -> p row u", u=2),
-                in_=turned_x[(c, half)][:].rearrange("p u row -> p row u"),
+                in_=turned_x[(c, first)][:].rearrange("p u row -> p row u"),
             )
 
-        def quantise_x(c):
-            codes = quantised.tile([P, CHUNK], U32, align_bytes=64)
-            plane = quantised.tile([P, CHUNK], U8, align_bytes=64)
-            nc.vector.quantize_mx(out=codes[:].bitcast(FP8X4), scales=plane[:], in_=grouped[c][:])
-            x_mx[c] = (codes, plane)
+        def quantise_x(c, first, tiles):
+            if first == 0:
+                codes = quantised.tile([P, CHUNK], U32, align_bytes=64)
+                plane = quantised.tile([P, CHUNK], U8, align_bytes=64)
+                x_mx[c] = (codes, plane)
+            codes, plane = x_mx[c]
+            rows = slice(first * P, (first + tiles) * P)
+            nc.vector.quantize_mx(
+                out=codes[:, rows].bitcast(FP8X4),
+                scales=plane[:, rows],
+                in_=grouped[c][:, first * P * PACK : (first + tiles) * P * PACK],
+            )
 
         def place(s):
             return s // COL_TILES, (s % COL_TILES) // 2, s % 2
 
-        def multiply(s):
+        def multiply(s, first=0, tiles=ROW_TILES):
             c, d, half = place(s)
             codes, plane = x_mx[c]
+            rows = slice(first * P, (first + tiles) * P)
             banks = []
-            for block in (I_BLOCK, G_BLOCK, O_BLOCK):
+            for place_in_tile, block in enumerate(USED_BLOCKS):
                 cols = slice(block * H + half * P, block * H + (half + 1) * P)
-                bank = gate_psum.tile([P, CHUNK], F32, tag="gate")
+                bank = gate_psum.tile([P, tiles * P], F32, tag="gate")
                 nc.tensor.matmul_mx(
                     out=bank[:],
-                    lhsT=w_codes[:, d, cols].bitcast(FP8X4),
+                    lhsT=w_codes[(d, half)][:, place_in_tile, :].bitcast(FP8X4),
                     lhsT_scale=w_planes[:, d, cols],
-                    rhs=codes[:].bitcast(FP8X4),
-                    rhs_scale=plane[:],
+                    rhs=codes[:, rows].bitcast(FP8X4),
+                    rhs_scale=plane[:, rows],
                     start=True,
                     stop=True,
                 )
                 banks.append(bank)
             gates[s] = banks
 
-        def activate_gates(s):
+        def activate_gates(s, first=0, tiles=ROW_TILES):
             c, d, half = place(s)
             bank_i, bank_g, bank_o = gates[s]
+            rows = slice(first * P, (first + tiles) * P)
 
             def bias_of(block):
                 t = (d * GATE_COLS + block * H + half * P) // P
                 return bias[:, t : t + 1]
 
-            s_i = work.tile([P, CHUNK], F32)
-            nc.scalar.activation(out=s_i[:], in_=bank_i[:], func=ACT.Sigmoid, bias=bias_of(I_BLOCK))
-            t_g = work.tile([P, CHUNK], F32)
-            nc.scalar.activation(out=t_g[:], in_=bank_g[:], func=ACT.Tanh, bias=bias_of(G_BLOCK))
-            s_o = held.tile([P, CHUNK], F32)
-            nc.scalar.activation(out=s_o[:], in_=bank_o[:], func=ACT.Sigmoid, bias=bias_of(O_BLOCK))
-            sig_i[s], tanh_g[s], sig_o[s] = s_i, t_g, s_o
+            if first == 0:
+                s_i = work.tile([P, CHUNK], F32)
+                t_g = work.tile([P, CHUNK], F32)
+                s_o = held.tile([P, CHUNK], F32)
+                sig_i[s], tanh_g[s], sig_o[s] = s_i, t_g, s_o
+            nc.scalar.activation(
+                out=sig_i[s][:, rows], in_=bank_i[:], func=ACT.Sigmoid, bias=bias_of(I_BLOCK)
+            )
+            nc.scalar.activation(
+                out=tanh_g[s][:, rows], in_=bank_g[:], func=ACT.Tanh, bias=bias_of(G_BLOCK)
+            )
+            nc.scalar.activation(
+                out=sig_o[s][:, rows], in_=bank_o[:], func=ACT.Sigmoid, bias=bias_of(O_BLOCK)
+            )
 
         def cell_state(s):
             c_new = work.tile([P, CHUNK], F32)
@@ -199,36 +223,39 @@ def tile_lstmnetwork_pa_t_e_kernel(tc, x, w_ih_words, w_ih_scales, b_ih, b_hh, o
             first_col = (s % COL_TILES) * P
             nc.sync.dma_start(out=out_rows[s // COL_TILES][:, :, first_col : first_col + P], in_=h_out[:])
 
-        transpose_x(0, 0)
-        transpose_x(0, 1)
         bias_turned = turn_psum.tile([P, P], F32, tag="turn")
         nc.tensor.transpose(bias_turned[:], bias_rows[:], ident[:])
-        regroup_x(0, 0)
-        regroup_x(0, 1)
         nc.vector.tensor_copy(out=bias[:], in_=bias_turned[:, 0:BIAS_ROWS])
-        quantise_x(0)
+        for first, tiles in FIRST_PIECES:
+            transpose_x(0, first, tiles)
+        for first, tiles in FIRST_PIECES:
+            regroup_x(0, first, tiles)
+            quantise_x(0, first, tiles)
+        for s, first, tiles in FIRST_GATES:
+            multiply(s, first, tiles)
+            activate_gates(s, first, tiles)
 
         for s in range(-1, STEPS + STORE_LAG):
-            next_chunk, piece = (s + 1) // COL_TILES + 1, (s + 1) % COL_TILES
-            prepare = next_chunk < CHUNKS
+            next_chunk, piece = s // COL_TILES + 1, s % COL_TILES
+            prepare = 0 <= s and next_chunk < CHUNKS
 
-            if 0 <= s < STEPS:
+            if 2 <= s < STEPS:
                 activate_gates(s)
             if 0 <= s - 1 < STEPS:
                 activate_cell(s - 1)
             if prepare and piece == 3:
-                quantise_x(next_chunk)
-            if s + 1 < STEPS:
+                quantise_x(next_chunk, 0, ROW_TILES)
+            if 2 <= s + 1 < STEPS:
                 multiply(s + 1)
             if 0 <= s - 2 < STEPS:
                 hidden_state(s - 2)
             if 0 <= s - STORE_LAG < STEPS:
                 store(s - STORE_LAG)
             if prepare and piece in (1, 2):
-                regroup_x(next_chunk, piece - 1)
+                regroup_x(next_chunk, 2 * (piece - 1), 2)
             if 0 <= s - 2 < STEPS:
                 transpose_h(s - 2)
             if prepare and piece in (0, 1):
-                transpose_x(next_chunk, piece)
+                transpose_x(next_chunk, 2 * piece, 2)
             if 0 <= s < STEPS:
                 cell_state(s)

@@ -108,7 +108,8 @@ def tile_lstmnetwork_pa_t_e_kernel(tc, x, w_ih_words, w_ih_scales, b_ih, b_hh, o
         grouped = {}
         x_mx = {}
         gates = {}
-        sig_i, tanh_g, sig_o, cell, tanh_c, hidden, turned_h = {}, {}, {}, {}, {}, {}, {}
+        sig_i, tanh_g, sig_o, cell, tanh_c, hidden, turned_h, staged = {}, {}, {}, {}, {}, {}, {}, {}
+        turned_c, turned_o = {}, {}
 
         def transpose_x(c, first, tiles):
             x_words = x_sb[(c, first // 2)][:].bitcast(F32)
@@ -169,7 +170,7 @@ def tile_lstmnetwork_pa_t_e_kernel(tc, x, w_ih_words, w_ih_scales, b_ih, b_hh, o
                 banks.append(bank)
             gates[s] = banks
 
-        def activate_gates(s, first=0, tiles=ROW_TILES):
+        def activate_gates(s, first=0, tiles=ROW_TILES, inner=True, outer=True):
             c, d, half = place(s)
             bank_i, bank_g, bank_o = gates[s]
             rows = slice(first * P, (first + tiles) * P)
@@ -178,25 +179,31 @@ def tile_lstmnetwork_pa_t_e_kernel(tc, x, w_ih_words, w_ih_scales, b_ih, b_hh, o
                 t = (d * GATE_COLS + block * H + half * P) // P
                 return bias[:, t : t + 1]
 
-            if first == 0:
+            if first == 0 and inner:
                 s_i = work.tile([P, CHUNK], F32)
                 t_g = work.tile([P, CHUNK], F32)
                 s_o = held.tile([P, CHUNK], F32)
                 sig_i[s], tanh_g[s], sig_o[s] = s_i, t_g, s_o
-            nc.scalar.activation(
-                out=sig_i[s][:, rows], in_=bank_i[:], func=ACT.Sigmoid, bias=bias_of(I_BLOCK)
-            )
-            nc.scalar.activation(
-                out=tanh_g[s][:, rows], in_=bank_g[:], func=ACT.Tanh, bias=bias_of(G_BLOCK)
-            )
-            nc.scalar.activation(
-                out=sig_o[s][:, rows], in_=bank_o[:], func=ACT.Sigmoid, bias=bias_of(O_BLOCK)
-            )
+            if inner:
+                nc.scalar.activation(
+                    out=sig_i[s][:, rows], in_=bank_i[:], func=ACT.Sigmoid, bias=bias_of(I_BLOCK)
+                )
+                nc.scalar.activation(
+                    out=tanh_g[s][:, rows], in_=bank_g[:], func=ACT.Tanh, bias=bias_of(G_BLOCK)
+                )
+            if outer:
+                nc.scalar.activation(
+                    out=sig_o[s][:, rows], in_=bank_o[:], func=ACT.Sigmoid, bias=bias_of(O_BLOCK)
+                )
 
-        def cell_state(s):
-            c_new = work.tile([P, CHUNK], F32)
-            nc.vector.tensor_tensor(out=c_new[:], in0=sig_i[s][:], in1=tanh_g[s][:], op=ALU.mult)
-            cell[s] = c_new
+        def cell_state(s, first=0, tiles=ROW_TILES):
+            if first == 0:
+                c_new = work.tile([P, CHUNK], F32)
+                cell[s] = c_new
+            rows = slice(first * P, (first + tiles) * P)
+            nc.vector.tensor_tensor(
+                out=cell[s][:, rows], in0=sig_i[s][:, rows], in1=tanh_g[s][:, rows], op=ALU.mult
+            )
 
         def activate_cell(s):
             t_c = work.tile([P, CHUNK], F32)
@@ -208,20 +215,49 @@ def tile_lstmnetwork_pa_t_e_kernel(tc, x, w_ih_words, w_ih_scales, b_ih, b_hh, o
             nc.vector.tensor_tensor(out=h_t[:], in0=sig_o[s][:], in1=tanh_c[s][:], op=ALU.mult)
             hidden[s] = h_t
 
-        def transpose_h(s):
-            h_rows = turn_psum.tile([P, ROW_TILES, P], F32, tag="turn")
-            for r in range(ROW_TILES):
-                nc.tensor.transpose(h_rows[:, r, :], hidden[s][:, r * P : (r + 1) * P], ident[:])
-            turned_h[s] = h_rows
+        def turn(kept, turned, s, first=0, tiles=ROW_TILES, in_gate_bank=False):
+            if in_gate_bank:
+                rows_first = gate_psum.tile([P, tiles, P], F32, tag="gate")
+            else:
+                rows_first = turn_psum.tile([P, tiles, P], F32, tag="turn")
+            for r in range(tiles):
+                nc.tensor.transpose(
+                    rows_first[:, r, :], kept[s][:, (first + r) * P : (first + r + 1) * P], ident[:]
+                )
+            turned[(s, first)] = rows_first
+
+        def send(s, first, tiles):
+            first_col = (s % COL_TILES) * P
+            nc.sync.dma_start(
+                out=out_rows[s // COL_TILES][:, first : first + tiles, first_col : first_col + P],
+                in_=staged[s][:, first : first + tiles, :],
+            )
 
         def store(s):
             h_out = stage.tile([P, ROW_TILES, P], F32)
-            if s < STEPS - STORE_LAG:
-                nc.vector.tensor_copy(out=h_out[:], in_=turned_h[s][:])
-            else:
-                nc.scalar.copy(out=h_out[:], in_=turned_h[s][:])
-            first_col = (s % COL_TILES) * P
-            nc.sync.dma_start(out=out_rows[s // COL_TILES][:, :, first_col : first_col + P], in_=h_out[:])
+            staged[s] = h_out
+            nc.vector.tensor_copy(out=h_out[:], in_=turned_h[(s, 0)][:])
+            send(s, 0, ROW_TILES)
+
+        def activate_turned_cell(s, first=0, tiles=ROW_TILES):
+            if first == 0:
+                t_c_rows = work.tile([P, ROW_TILES, P], F32)
+                tanh_c[s] = t_c_rows
+            nc.scalar.activation(
+                out=tanh_c[s][:, first : first + tiles, :], in_=turned_c[(s, first)][:], func=ACT.Tanh
+            )
+
+        def finish(s, first=0, tiles=ROW_TILES):
+            if first == 0:
+                h_out = stage.tile([P, ROW_TILES, P], F32)
+                staged[s] = h_out
+            nc.vector.tensor_tensor(
+                out=staged[s][:, first : first + tiles, :],
+                in0=turned_o[(s, first)][:],
+                in1=tanh_c[s][:, first : first + tiles, :],
+                op=ALU.mult,
+            )
+            send(s, first, tiles)
 
         bias_turned = turn_psum.tile([P, P], F32, tag="turn")
         nc.tensor.transpose(bias_turned[:], bias_rows[:], ident[:])
@@ -235,27 +271,48 @@ def tile_lstmnetwork_pa_t_e_kernel(tc, x, w_ih_words, w_ih_scales, b_ih, b_hh, o
             multiply(s, first, tiles)
             activate_gates(s, first, tiles)
 
-        for s in range(-1, STEPS + STORE_LAG):
+        last = STEPS - 1
+        short_from = STEPS - COL_TILES
+        for s in range(-1, STEPS):
             next_chunk, piece = s // COL_TILES + 1, s % COL_TILES
             prepare = 0 <= s and next_chunk < CHUNKS
 
-            if 2 <= s < STEPS:
-                activate_gates(s)
-            if 0 <= s - 1 < STEPS:
+            if short_from <= s - 1:
+                turn(cell, turned_c, s - 1)
+                turn(sig_o, turned_o, s - 1)
+            if 2 <= s:
+                activate_gates(s, outer=False)
+            if 0 <= s - 1 < short_from:
                 activate_cell(s - 1)
+            if short_from <= s - 1:
+                activate_turned_cell(s - 1)
+            if 2 <= s:
+                activate_gates(s, inner=False)
             if prepare and piece == 3:
                 quantise_x(next_chunk, 0, ROW_TILES)
-            if 2 <= s + 1 < STEPS:
+            if 2 <= s + 1 <= last:
                 multiply(s + 1)
-            if 0 <= s - 2 < STEPS:
+            if 0 <= s - 2 < short_from:
                 hidden_state(s - 2)
-            if 0 <= s - STORE_LAG < STEPS:
+            if 0 <= s - STORE_LAG < short_from:
                 store(s - STORE_LAG)
             if prepare and piece in (1, 2):
                 regroup_x(next_chunk, 2 * (piece - 1), 2)
-            if 0 <= s - 2 < STEPS:
-                transpose_h(s - 2)
+            if 0 <= s - 2 < short_from:
+                turn(hidden, turned_h, s - 2)
             if prepare and piece in (0, 1):
                 transpose_x(next_chunk, 2 * piece, 2)
-            if 0 <= s < STEPS:
+            if 0 <= s < last:
                 cell_state(s)
+            if s == last:
+                for r in range(ROW_TILES):
+                    cell_state(last, r, 1)
+                    turn(cell, turned_c, last, r, 1, in_gate_bank=True)
+            if short_from <= s - 1:
+                finish(s - 1)
+
+        for r in range(ROW_TILES):
+            turn(sig_o, turned_o, last, r, 1)
+        for r in range(ROW_TILES):
+            activate_turned_cell(last, r, 1)
+            finish(last, r, 1)

@@ -29,6 +29,7 @@ COL_TILES = DIRS * H // P
 STEPS = CHUNKS * COL_TILES
 STORE_LAG = 3
 BIAS_ROWS = DIRS * GATE_COLS // P
+WARM_UPS = 4
 FIRST_PIECES = ((0, 1), (1, 1), (2, 2))
 FIRST_GATES = ((0, 0, 1), (0, 1, 1), (1, 0, 2), (0, 2, 2), (1, 2, 2))
 
@@ -51,6 +52,12 @@ def tile_lstmnetwork_pa_t_e_kernel(tc, x, w_ih_words, w_ih_scales, b_ih, b_hh, o
         stage = ctx.enter_context(tc.tile_pool(name="stage", bufs=4))
         gate_psum = ctx.enter_context(tc.psum_pool(name="gate_psum", bufs=5))
         turn_psum = ctx.enter_context(tc.psum_pool(name="turn_psum", bufs=3))
+
+        zeros = const.tile([P, CHUNK], BF16)
+        nc.gpsimd.memset(zeros[:], 0.0)
+        idle_bank = gate_psum.tile([P, CHUNK], F32, tag="gate")
+        for warm_up in range(WARM_UPS):
+            nc.tensor.matmul(idle_bank[:], lhsT=zeros[:, 0:P], rhs=zeros[:], start=True, stop=True)
 
         x_sb = {}
 

@@ -29,6 +29,7 @@ COL_TILES = DIRS * H // P
 STEPS = CHUNKS * COL_TILES
 STORE_LAG = 3
 BIAS_ROWS = DIRS * GATE_COLS // P
+LAST_HALVES = (0, 2)
 WARM_UPS = 4
 FIRST_PIECES = ((0, 1), (1, 1), (2, 2))
 FIRST_GATES = ((0, 0, 1), (0, 1, 1), (1, 0, 2), (0, 2, 2), (1, 2, 2))
@@ -175,12 +176,13 @@ def tile_lstmnetwork_pa_t_e_kernel(tc, x, w_ih_words, w_ih_scales, b_ih, b_hh, o
                     stop=True,
                 )
                 banks.append(bank)
-            gates[s] = banks
+            gates[s] = (banks, first)
 
         def activate_gates(s, first=0, tiles=ROW_TILES, inner=True, outer=True):
             c, d, half = place(s)
-            bank_i, bank_g, bank_o = gates[s]
+            (bank_i, bank_g, bank_o), bank_first = gates[s]
             rows = slice(first * P, (first + tiles) * P)
+            in_bank = slice((first - bank_first) * P, (first - bank_first + tiles) * P)
 
             def bias_of(block):
                 t = (d * GATE_COLS + block * H + half * P) // P
@@ -193,14 +195,14 @@ def tile_lstmnetwork_pa_t_e_kernel(tc, x, w_ih_words, w_ih_scales, b_ih, b_hh, o
                 sig_i[s], tanh_g[s], sig_o[s] = s_i, t_g, s_o
             if inner:
                 nc.scalar.activation(
-                    out=sig_i[s][:, rows], in_=bank_i[:], func=ACT.Sigmoid, bias=bias_of(I_BLOCK)
+                    out=sig_i[s][:, rows], in_=bank_i[:, in_bank], func=ACT.Sigmoid, bias=bias_of(I_BLOCK)
                 )
                 nc.scalar.activation(
-                    out=tanh_g[s][:, rows], in_=bank_g[:], func=ACT.Tanh, bias=bias_of(G_BLOCK)
+                    out=tanh_g[s][:, rows], in_=bank_g[:, in_bank], func=ACT.Tanh, bias=bias_of(G_BLOCK)
                 )
             if outer:
                 nc.scalar.activation(
-                    out=sig_o[s][:, rows], in_=bank_o[:], func=ACT.Sigmoid, bias=bias_of(O_BLOCK)
+                    out=sig_o[s][:, rows], in_=bank_o[:, in_bank], func=ACT.Sigmoid, bias=bias_of(O_BLOCK)
                 )
 
         def cell_state(s, first=0, tiles=ROW_TILES):
@@ -293,7 +295,7 @@ def tile_lstmnetwork_pa_t_e_kernel(tc, x, w_ih_words, w_ih_scales, b_ih, b_hh, o
                 activate_cell(s - 1)
             if short_from <= s - 1:
                 activate_turned_cell(s - 1)
-            if 2 <= s:
+            if 2 <= s < last:
                 activate_gates(s, inner=False)
             if prepare and piece == 3:
                 quantise_x(next_chunk, 0, ROW_TILES)
@@ -312,14 +314,15 @@ def tile_lstmnetwork_pa_t_e_kernel(tc, x, w_ih_words, w_ih_scales, b_ih, b_hh, o
             if 0 <= s < last:
                 cell_state(s)
             if s == last:
-                for r in range(ROW_TILES):
-                    cell_state(last, r, 1)
-                    turn(cell, turned_c, last, r, 1, in_gate_bank=True)
+                for first in LAST_HALVES:
+                    cell_state(last, first, 2)
+                    turn(cell, turned_c, last, first, 2, in_gate_bank=True)
+                for first in LAST_HALVES:
+                    activate_gates(last, first, 2, inner=False)
+                    turn(sig_o, turned_o, last, first, 2)
             if short_from <= s - 1:
                 finish(s - 1)
 
-        for r in range(ROW_TILES):
-            turn(sig_o, turned_o, last, r, 1)
-        for r in range(ROW_TILES):
-            activate_turned_cell(last, r, 1)
-            finish(last, r, 1)
+        for first in LAST_HALVES:
+            activate_turned_cell(last, first, 2)
+            finish(last, first, 2)

from contextlib import ExitStack

import concourse.mybir as mybir
from concourse.masks import make_identity

F32 = mybir.dt.float32
BF16 = mybir.dt.bfloat16
I32 = mybir.dt.int32
U32 = mybir.dt.uint32
U8 = mybir.dt.uint8
FP8X4 = mybir.dt.float8_e4m3fn_x4
ACT = mybir.ActivationFunctionType
ALU = mybir.AluOpType

P = 128
PACK = 4
K = P * PACK
PAIRS = K // 2
ROWS = 4096
CHUNK = 512
ROW_TILES = CHUNK // P
CHUNKS = ROWS // CHUNK
DIRS = 2
H = 256
GATE_COLS = 4 * H
I_BLOCK, G_BLOCK, O_BLOCK = 0, 2, 3
USED_BLOCKS = (I_BLOCK, G_BLOCK, O_BLOCK)
COL_TILES = DIRS * H // P
STEPS = CHUNKS * COL_TILES
STORE_LAG = 3
BIAS_ROWS = DIRS * GATE_COLS // P
LAST_HALVES = (0, 2)
WARM_UPS = 4
FIRST_PIECES = ((0, 1), (1, 1), (2, 2))
FIRST_GATES = ((0, 0, 1), (0, 1, 1), (1, 0, 2), (0, 2, 2), (1, 2, 2))

FLOPS = 2 * ROWS * K * DIRS * 3 * H
BYTES = ROWS * K * 2 + DIRS * 3 * H * (K + K // 32 + 2 * 2) + ROWS * DIRS * H * 4


def tile_lstmnetwork_pa_t_e_kernel(tc, x, w_ih_words, w_ih_scales, b_ih, b_hh, out):
    nc = tc.nc

    x_rows = x.rearrange("b c k -> (b c) k").rearrange("(c p r) k -> c p (r k)", p=P, r=ROW_TILES)
    out_rows = out.rearrange("(c p r) n -> c p r n", p=P, r=ROW_TILES)

    with ExitStack() as ctx:
        ctx.enter_context(tc.manual_schedule())
        const = ctx.enter_context(tc.tile_pool(name="const", bufs=1))
        quantised = ctx.enter_context(tc.tile_pool(name="quantised", bufs=2))
        work = ctx.enter_context(tc.tile_pool(name="work", bufs=2))
        held = ctx.enter_context(tc.tile_pool(name="held", bufs=3))
        stage = ctx.enter_context(tc.tile_pool(name="stage", bufs=4))
        gate_psum = ctx.enter_context(tc.psum_pool(name="gate_psum", bufs=5))
        turn_psum = ctx.enter_context(tc.psum_pool(name="turn_psum", bufs=3))

        zeros = const.tile([P, CHUNK], BF16)
        nc.gpsimd.memset(zeros[:], 0.0)
        idle_bank = gate_psum.tile([P, CHUNK], F32, tag="gate")
        for warm_up in range(WARM_UPS):
            nc.tensor.matmul(idle_bank[:], lhsT=zeros[:, 0:P], rhs=zeros[:], start=True, stop=True)

        x_sb = {}

        def load_x(c, half):
            x_half = const.tile([P, 2 * K], BF16, name="x_%d_%d" % (c, half))
            nc.sync.dma_start(out=x_half[:], in_=x_rows[c][:, half * 2 * K : (half + 1) * 2 * K])
            x_sb[(c, half)] = x_half

        b_ih_rows = const.tile([BIAS_ROWS, P], BF16)
        b_hh_rows = const.tile([BIAS_ROWS, P], BF16)
        nc.sync.dma_start(out=b_ih_rows[:], in_=b_ih.rearrange("d (t c) -> (d t) c", c=P))
        nc.sync.dma_start(out=b_hh_rows[:], in_=b_hh.rearrange("d (t c) -> (d t) c", c=P))

        load_x(0, 0)
        load_x(0, 1)

        w_planes = const.tile([P, DIRS, GATE_COLS], U8, align_bytes=64)
        nc.vector.memset(w_planes[:].bitcast(I32), 0)
        scale_rows = w_ih_scales.rearrange("d q n -> q d n")
        for quadrant in range(4):
            nc.sync.dma_start(
                out=w_planes[32 * quadrant : 32 * quadrant + 4, :, :].bitcast(I32),
                in_=scale_rows[4 * quadrant : 4 * quadrant + 4].bitcast(I32),
            )

        w_codes = {}

        def load_codes(d, half):
            codes = const.tile([P, len(USED_BLOCKS), P], U32, name="w_%d_%d" % (d, half), align_bytes=64)
            blocks_dram = w_ih_words[d].rearrange("p n t -> p (n t)").bitcast(I32).rearrange("p (b n) -> p b n", n=H)
            cols = slice(half * P, (half + 1) * P)
            nc.sync.dma_start(out=codes[:, 0, :].bitcast(I32), in_=blocks_dram[:, I_BLOCK, cols])
            nc.sync.dma_start(out=codes[:, 1:3, :].bitcast(I32), in_=blocks_dram[:, G_BLOCK : O_BLOCK + 1, cols])
            w_codes[(d, half)] = codes

        load_codes(0, 0)
        load_codes(0, 1)
        load_codes(1, 0)
        load_codes(1, 1)
        for c in range(1, CHUNKS):
            load_x(c, 0)
            load_x(c, 1)

        ident = const.tile([P, P], F32)
        make_identity(nc, ident[:])

        bias_rows = const.tile([P, P], F32)
        nc.vector.memset(bias_rows[:], 0.0)
        nc.vector.tensor_tensor(
            out=bias_rows[0:BIAS_ROWS, :], in0=b_ih_rows[:], in1=b_hh_rows[:], op=ALU.add
        )
        bias = const.tile([P, BIAS_ROWS], F32)

        turned_x = {}
        grouped = {}
        x_mx = {}
        gates = {}
        sig_i, tanh_g, sig_o, cell, tanh_c, hidden, turned_h, staged = {}, {}, {}, {}, {}, {}, {}, {}
        turned_c, turned_o = {}, {}

        def transpose_x(c, first, tiles):
            x_words = x_sb[(c, first // 2)][:].bitcast(F32)
            planes = turn_psum.tile([P, 2, tiles * P], F32, tag="turn")
            for t in range(tiles):
                first_word = ((first + t) % 2) * PAIRS
                for u in range(2):
                    nc.tensor.transpose(
                        planes[:, u, t * P : (t + 1) * P],
                        x_words[:, first_word + u : first_word + PAIRS : 2],
                        ident[:],
                    )
            turned_x[(c, first)] = planes

        def regroup_x(c, first, tiles):
            if first == 0:
                in_order = quantised.tile([P, CHUNK * PACK], BF16, align_bytes=64)
                grouped[c] = in_order
            words = grouped[c][:].bitcast(F32)[:, first * 2 * P : (first + tiles) * 2 * P]
            nc.vector.tensor_copy(
                out=words.rearrange("p (row u) -> p row u", u=2),
                in_=turned_x[(c, first)][:].rearrange("p u row -> p row u"),
            )

        def quantise_x(c, first, tiles):
            if first == 0:
                codes = quantised.tile([P, CHUNK], U32, align_bytes=64)
                plane = quantised.tile([P, CHUNK], U8, align_bytes=64)
                x_mx[c] = (codes, plane)
            codes, plane = x_mx[c]
            rows = slice(first * P, (first + tiles) * P)
            nc.vector.quantize_mx(
                out=codes[:, rows].bitcast(FP8X4),
                scales=plane[:, rows],
                in_=grouped[c][:, first * P * PACK : (first + tiles) * P * PACK],
            )

        def place(s):
            return s // COL_TILES, (s % COL_TILES) // 2, s % 2

        def multiply(s, first=0, tiles=ROW_TILES):
            c, d, half = place(s)
            codes, plane = x_mx[c]
            rows = slice(first * P, (first + tiles) * P)
            banks = []
            for place_in_tile, block in enumerate(USED_BLOCKS):
                cols = slice(block * H + half * P, block * H + (half + 1) * P)
                bank = gate_psum.tile([P, tiles * P], F32, tag="gate")
                nc.tensor.matmul_mx(
                    out=bank[:],
                    lhsT=w_codes[(d, half)][:, place_in_tile, :].bitcast(FP8X4),
                    lhsT_scale=w_planes[:, d, cols],
                    rhs=codes[:, rows].bitcast(FP8X4),
                    rhs_scale=plane[:, rows],
                    start=True,
                    stop=True,
                )
                banks.append(bank)
            gates[s] = (banks, first)

        def activate_gates(s, first=0, tiles=ROW_TILES, inner=True, outer=True):
            c, d, half = place(s)
            (bank_i, bank_g, bank_o), bank_first = gates[s]
            rows = slice(first * P, (first + tiles) * P)
            in_bank = slice((first - bank_first) * P, (first - bank_first + tiles) * P)

            def bias_of(block):
                t = (d * GATE_COLS + block * H + half * P) // P
                return bias[:, t : t + 1]

            if first == 0 and inner:
                s_i = work.tile([P, CHUNK], F32)
                t_g = work.tile([P, CHUNK], F32)
                s_o = held.tile([P, CHUNK], F32)
                sig_i[s], tanh_g[s], sig_o[s] = s_i, t_g, s_o
            if inner:
                nc.scalar.activation(
                    out=sig_i[s][:, rows], in_=bank_i[:, in_bank], func=ACT.Sigmoid, bias=bias_of(I_BLOCK)
                )
                nc.scalar.activation(
                    out=tanh_g[s][:, rows], in_=bank_g[:, in_bank], func=ACT.Tanh, bias=bias_of(G_BLOCK)
                )
            if outer:
                nc.scalar.activation(
                    out=sig_o[s][:, rows], in_=bank_o[:, in_bank], func=ACT.Sigmoid, bias=bias_of(O_BLOCK)
                )

        def cell_state(s, first=0, tiles=ROW_TILES):
            if first == 0:
                c_new = work.tile([P, CHUNK], F32)
                cell[s] = c_new
            rows = slice(first * P, (first + tiles) * P)
            nc.vector.tensor_tensor(
                out=cell[s][:, rows], in0=sig_i[s][:, rows], in1=tanh_g[s][:, rows], op=ALU.mult
            )

        def activate_cell(s):
            t_c = work.tile([P, CHUNK], F32)
            nc.scalar.activation(out=t_c[:], in_=cell[s][:], func=ACT.Tanh)
            tanh_c[s] = t_c

        def hidden_state(s):
            h_t = work.tile([P, CHUNK], F32)
            nc.vector.tensor_tensor(out=h_t[:], in0=sig_o[s][:], in1=tanh_c[s][:], op=ALU.mult)
            hidden[s] = h_t

        def turn(kept, turned, s, first=0, tiles=ROW_TILES, in_gate_bank=False):
            if in_gate_bank:
                rows_first = gate_psum.tile([P, tiles, P], F32, tag="gate")
            else:
                rows_first = turn_psum.tile([P, tiles, P], F32, tag="turn")
            for r in range(tiles):
                nc.tensor.transpose(
                    rows_first[:, r, :], kept[s][:, (first + r) * P : (first + r + 1) * P], ident[:]
                )
            turned[(s, first)] = rows_first

        def send(s, first, tiles):
            first_col = (s % COL_TILES) * P
            nc.sync.dma_start(
                out=out_rows[s // COL_TILES][:, first : first + tiles, first_col : first_col + P],
                in_=staged[s][:, first : first + tiles, :],
            )

        def store(s):
            h_out = stage.tile([P, ROW_TILES, P], F32)
            staged[s] = h_out
            nc.vector.tensor_copy(out=h_out[:], in_=turned_h[(s, 0)][:])
            send(s, 0, ROW_TILES)

        def activate_turned_cell(s, first=0, tiles=ROW_TILES):
            if first == 0:
                t_c_rows = work.tile([P, ROW_TILES, P], F32)
                tanh_c[s] = t_c_rows
            nc.scalar.activation(
                out=tanh_c[s][:, first : first + tiles, :], in_=turned_c[(s, first)][:], func=ACT.Tanh
            )

        def finish(s, first=0, tiles=ROW_TILES):
            if first == 0:
                h_out = stage.tile([P, ROW_TILES, P], F32)
                staged[s] = h_out
            nc.vector.tensor_tensor(
                out=staged[s][:, first : first + tiles, :],
                in0=turned_o[(s, first)][:],
                in1=tanh_c[s][:, first : first + tiles, :],
                op=ALU.mult,
            )
            send(s, first, tiles)

        bias_turned = turn_psum.tile([P, P], F32, tag="turn")
        nc.tensor.transpose(bias_turned[:], bias_rows[:], ident[:])
        nc.vector.tensor_copy(out=bias[:], in_=bias_turned[:, 0:BIAS_ROWS])
        for first, tiles in FIRST_PIECES:
            transpose_x(0, first, tiles)
        for first, tiles in FIRST_PIECES:
            regroup_x(0, first, tiles)
            quantise_x(0, first, tiles)
        for s, first, tiles in FIRST_GATES:
            multiply(s, first, tiles)
            activate_gates(s, first, tiles)

        last = STEPS - 1
        short_from = STEPS - COL_TILES
        for s in range(-1, STEPS):
            next_chunk, piece = s // COL_TILES + 1, s % COL_TILES
            prepare = 0 <= s and next_chunk < CHUNKS

            if short_from <= s - 1:
                turn(cell, turned_c, s - 1)
                turn(sig_o, turned_o, s - 1)
            if 2 <= s:
                activate_gates(s, outer=False)
            if 0 <= s - 1 < short_from:
                activate_cell(s - 1)
            if short_from <= s - 1:
                activate_turned_cell(s - 1)
            if 2 <= s < last:
                activate_gates(s, inner=False)
            if prepare and piece == 3:
                quantise_x(next_chunk, 0, ROW_TILES)
            if 2 <= s + 1 <= last:
                multiply(s + 1)
            if 0 <= s - 2 < short_from:
                hidden_state(s - 2)
            if 0 <= s - STORE_LAG < short_from:
                store(s - STORE_LAG)
            if prepare and piece in (1, 2):
                regroup_x(next_chunk, 2 * (piece - 1), 2)
            if 0 <= s - 2 < short_from:
                turn(hidden, turned_h, s - 2)
            if prepare and piece in (0, 1):
                transpose_x(next_chunk, 2 * piece, 2)
            if 0 <= s < last:
                cell_state(s)
            if s == last:
                for first in LAST_HALVES:
                    cell_state(last, first, 2)
                    turn(cell, turned_c, last, first, 2, in_gate_bank=True)
                for first in LAST_HALVES:
                    activate_gates(last, first, 2, inner=False)
                    turn(sig_o, turned_o, last, first, 2)
            if short_from <= s - 1:
                finish(s - 1)

        for first in LAST_HALVES:
            activate_turned_cell(last, first, 2)
            finish(last, first, 2)
